import numpy as np
import ml_dtypes


def mxq(x, axis, fmt="e4m3"):
    dtype, down = {"e4m3": (ml_dtypes.float8_e4m3fn, 7), "e5m2": (ml_dtypes.float8_e5m2, 14)}[fmt]
    v = np.moveaxis(np.asarray(x, np.float32).astype(ml_dtypes.bfloat16).astype(np.float64), axis, -1)
    blocks = v.reshape(v.shape[:-1] + (-1, 32))
    amax = np.abs(blocks).max(-1, keepdims=True)
    byte = np.maximum(np.where(amax > 0, np.frexp(amax)[1] - 1 + 127, 0) - down, 1)
    scale = np.exp2(byte - 127.0)
    codes = (blocks / scale).astype(np.float32).astype(dtype).astype(np.float64)
    return np.moveaxis((codes * scale).reshape(v.shape), -1, axis)


WIDE = False


def mx_kscale(k):
    if not WIDE:
        return np.ones(k)
    levels = np.array([20, -20, 10, -10, 0])
    a = np.random.permutation(np.resize(levels, k // 512 * 4)).reshape(k // 512, 4)
    idx = np.arange(k)
    return np.exp2(a[idx // 512, idx % 128 // 32])


BF16 = ml_dtypes.bfloat16


def bf(x):
    return np.asarray(x, np.float32).astype(BF16)


def f64(x):
    return np.asarray(x).astype(np.float64)


B, N, D = 4, 2, 512


def select_func(A1):
    return np.mean(np.abs(A1), axis=(-2, -1), keepdims=True) > 1.0


def reset_func(A1):
    return A1 / np.max(np.abs(A1), axis=(-2, -1), keepdims=True)


def reset_left(left):
    A1 = left[..., :D, :]
    B1 = left[..., D:, :]
    is_selected = select_func(A1)
    bias_is_unmodified = np.all(B1 == 0, axis=(-2, -1), keepdims=True)
    should_reset = is_selected & bias_is_unmodified
    A1_new = np.where(should_reset, reset_func(A1), A1)
    B1_new = np.where(should_reset, np.zeros_like(B1), B1)
    return A1_new, B1_new


def setup_inputs():
    s = mx_kscale(D)
    c = np.exp2(np.round(np.log2(s.mean())))
    kind = np.random.permutation(np.arange(B) % 4).reshape(B, 1, 1, 1)
    large = kind < 2
    zero_bias = kind % 2 == 0
    scale = np.where(large, np.random.uniform(2.2, 3.0, (B, 1, 1, 1)), np.random.uniform(0.3, 0.6, (B, 1, 1, 1)))
    A1 = np.random.standard_normal((B, 1, D, D)) * scale * s[:, None] / c
    B1 = np.random.standard_normal((B, 1, D, D)) * 0.7 * np.where(zero_bias, 0.0, 1.0)
    A2 = np.random.standard_normal((B, N, D, D)) * 1.5 / np.sqrt(D)
    B2 = np.random.standard_normal((B, N, D, D))
    r = np.where(large & zero_bias, s.max() / c, 1.0)
    G = np.random.standard_normal((B, N, 2 * D, D)) * np.exp2(np.random.randint(-12, 1, (B, N, 2 * D, 1)))
    Gt = G[..., :D, :] * r * c / s[:, None]
    Gb = G[..., D:, :]
    return {"A1_atop_B1": bf(np.concatenate([A1, B1], axis=-2)),
            "A2_atop_B2": bf(np.concatenate([A2, B2], axis=-2)),
            "grad_out": bf(np.concatenate([Gt, Gb], axis=-2))}


def reference(A1_atop_B1, A2_atop_B2, grad_out):
    A1_new, B1_new = reset_left(f64(A1_atop_B1))
    top = np.concatenate([A1_new, B1_new], axis=-2)
    G = f64(grad_out)
    dA2 = np.swapaxes(mxq(top, 2, "e4m3"), -1, -2) @ mxq(G, 2, "e5m2")
    return np.concatenate([dA2, G[..., D:, :]], axis=-2)

@@ -1,0 +1,179 @@
+from contextlib import ExitStack
+
+import concourse.mybir as mybir
+from concourse.masks import make_identity
+
+FLOPS = 2 * 4 * 2 * 512 * 1024 * 512
+BYTES = 4 * 1024 * 512 * 2 + 8 * 1024 * 512 * 2 + 8 * 1024 * 512 * 4
+
+BF16 = mybir.dt.bfloat16
+F32 = mybir.dt.float32
+U32 = mybir.dt.uint32
+U8 = mybir.dt.uint8
+E4 = mybir.dt.float8_e4m3fn_x4
+E5 = mybir.dt.float8_e5m2_x4
+ALU = mybir.AluOpType
+ACT = mybir.ActivationFunctionType
+AX = mybir.AxisListType
+
+P = 128
+D = 512
+B = 4
+N = 2
+W = 4 * D
+FLT_MAX = 3.4028234663852886e38
+
+
+def tile_updateonrightwithselectiveresetonleft_kernel(tc, A1_atop_B1, A2_atop_B2, grad_out, out):
+    nc = tc.nc
+    with ExitStack() as ctx:
+        const = ctx.enter_context(tc.tile_pool(name="const", bufs=1))
+        rawp = ctx.enter_context(tc.tile_pool(name="raw", bufs=1))
+        scrp = ctx.enter_context(tc.tile_pool(name="scr", bufs=3))
+        small = ctx.enter_context(tc.tile_pool(name="small", bufs=2))
+        grpp = ctx.enter_context(tc.tile_pool(name="grp", bufs=5))
+        topq = ctx.enter_context(tc.tile_pool(name="topq", bufs=2))
+        gq = ctx.enter_context(tc.tile_pool(name="gq", bufs=3))
+        outp = ctx.enter_context(tc.tile_pool(name="outp", bufs=8))
+        accp = ctx.enter_context(tc.psum_pool(name="accp", bufs=6))
+        pstat = ctx.enter_context(tc.psum_pool(name="pstat", bufs=2))
+
+        raw_top = []
+        raw_g = []
+        for b in range(B):
+            rt = rawp.tile([P, 2, 4, D], BF16, name="rt%d" % b)
+            raw_top.append(rt)
+            for c in range(2):
+                nc.sync.dma_start(
+                    out=rt[:, c],
+                    in_=A1_atop_B1[b, 0, c * D:(c + 1) * D, :].rearrange("(p j) w -> p j w", j=4),
+                )
+            row = []
+            for n in range(N):
+                rg = rawp.tile([P, 2, 4, D], BF16, name="rg%d%d" % (b, n))
+                row.append(rg)
+                for c in (1, 0):
+                    nc.sync.dma_start(
+                        out=rg[:, c],
+                        in_=grad_out[b, n, c * D:(c + 1) * D, :].rearrange("(p j) w -> p j w", j=4),
+                    )
+            raw_g.append(row)
+
+        ident = const.tile([P, P], F32, name="ident")
+        make_identity(nc, ident[:])
+
+        factor = {}
+
+        def stats(b):
+            rt = raw_top[b]
+            abs_a = scrp.tile([P, W], BF16, name="abs_a", tag="scr")
+            sum_a = small.tile([P, 1], F32, name="sum_a")
+            nc.scalar.activation(out=abs_a[:], in_=rt[:, 0].rearrange("p j w -> p (j w)"), func=ACT.Abs,
+                                 accum_out=sum_a[:])
+            vstat = small.tile([P, 2], F32, name="vstat")
+            junk = scrp.tile([P, W], BF16, name="junk", tag="scr")
+            nc.vector.tensor_scalar(out=junk[:], in0=rt[:, 1].rearrange("p j w -> p (j w)"), scalar1=0.0,
+                                    scalar2=None, op0=ALU.not_equal, op1=ALU.max, accum_out=vstat[:, 1:2])
+            nc.vector.tensor_scalar(out=abs_a[:], in0=abs_a[:], scalar1=1.0, scalar2=None, op0=ALU.mult,
+                                    op1=ALU.max, accum_out=vstat[:, 0:1])
+            ps = pstat.tile([P, 3, P], F32, name="ps")
+            nc.tensor.transpose(out=ps[:, 0, :], in_=vstat[:, 0:1].to_broadcast([P, P]), identity=ident[:])
+            nc.tensor.transpose(out=ps[:, 1, :], in_=vstat[:, 1:2].to_broadcast([P, P]), identity=ident[:])
+            nc.tensor.transpose(out=ps[:, 2, :], in_=sum_a[:, 0:1].to_broadcast([P, P]), identity=ident[:])
+            red = small.tile([P, 2], F32, name="red")
+            nc.vector.tensor_reduce(out=red[:], in_=ps[:, 0:2, :], axis=AX.X, op=ALU.max)
+            tot = small.tile([P, 1], F32, name="tot")
+            nc.vector.tensor_reduce(out=tot[:], in_=ps[:, 2, :], axis=AX.X, op=ALU.add)
+            u = small.tile([P, 1], F32, name="u")
+            nc.vector.tensor_scalar(out=u[:], in0=red[:, 1:2], scalar1=0.0, scalar2=tot[:, 0:1],
+                                    op0=ALU.is_equal, op1=ALU.mult)
+            h = small.tile([P, 1], F32, name="h")
+            nc.vector.tensor_scalar(out=h[:], in0=u[:], scalar1=float(D * D), scalar2=FLT_MAX,
+                                    op0=ALU.is_gt, op1=ALU.mult)
+            g = small.tile([P, 1], F32, name="g")
+            nc.vector.tensor_scalar(out=g[:], in0=u[:], scalar1=float(D * D), scalar2=None, op0=ALU.is_le)
+            den = small.tile([P, 1], F32, name="den")
+            nc.vector.scalar_tensor_tensor(out=den[:], in0=red[:, 0:1], scalar=h[:, 0:1], in1=g[:],
+                                           op0=ALU.min, op1=ALU.max)
+            f = small.tile([P, 1], F32, name="f")
+            nc.vector.reciprocal(out=f[:], in_=den[:])
+            factor[b] = f
+
+        pending = []
+
+        def flush():
+            while pending:
+                pending.pop(0)()
+
+        def unit(eng, src, dst_view, src_view, grp, codes, scales, fmt, scale=None):
+            if eng == "v":
+                if scale is None:
+                    nc.vector.tensor_copy(out=dst_view, in_=src_view)
+                else:
+                    nc.vector.tensor_scalar(out=dst_view, in0=src_view, scalar1=scale, scalar2=None, op0=ALU.mult)
+            else:
+                if scale is None:
+                    nc.scalar.copy(out=dst_view, in_=src_view)
+                else:
+                    nc.scalar.activation(out=dst_view, in_=src_view, func=ACT.Copy, scale=scale)
+            flush()
+
+            def quant():
+                nc.vector.quantize_mx(out=codes.bitcast(fmt), scales=scales, in_=grp)
+            pending.append(quant)
+
+        def prep_top(b, c, eng, tq, ts):
+            grp = grpp.tile([P, 4, P, 4], BF16, name="grp_t", tag="grp", align_bytes=64)
+            unit(eng, None,
+                 grp[:].rearrange("p m i j -> p i j m"),
+                 raw_top[b][:, c].rearrange("p j (i m) -> p i j m", m=4),
+                 grp[:].rearrange("p m i j -> p (m i j)"),
+                 tq[:, c, :], ts[:, c, :], E4,
+                 scale=(factor[b][:, 0:1] if c == 0 else None))
+
+        def prep_g(b, n, c, eng, cq, cs):
+            grp = grpp.tile([P, D, 4], BF16, name="grp_g", tag="grp", align_bytes=64)
+            unit(eng, None,
+                 grp[:].rearrange("p (c i) t -> p c t i", i=4),
+                 raw_g[b][n][:, c].rearrange("p t (c i) -> p c t i", i=4),
+                 grp[:].rearrange("p w t -> p (w t)"),
+                 cq[:, c, :], cs[:, c, :], E5)
+
+        def cast(b, n):
+            ot = outp.tile([P, 4, D], F32, name="ot_c", tag="ot")
+            nc.vector.tensor_copy(out=ot[:], in_=raw_g[b][n][:, 1])
+            nc.sync.dma_start(out=out[b, n, D:2 * D, :].rearrange("(p j) w -> p j w", j=4), in_=ot[:])
+
+        def mm(b, n, tq, ts, cq, cs):
+            ot = outp.tile([P, 4, D], F32, name="ot_m", tag="ot")
+            for m in range(4):
+                acc = accp.tile([P, D], F32, name="acc")
+                for k, c in enumerate((1, 0)):
+                    nc.tensor.matmul_mx(
+                        out=acc[:],
+                        lhsT=tq[:, c, m * P:(m + 1) * P].bitcast(E4),
+                        lhsT_scale=ts[:, c, m * P:(m + 1) * P],
+                        rhs=cq[:, c, :].bitcast(E5),
+                        rhs_scale=cs[:, c, :],
+                        start=(k == 0),
+                        stop=(k == 1),
+                    )
+                nc.scalar.copy(out=ot[:, m, :], in_=acc[:])
+            nc.sync.dma_start(out=out[b, n, 0:D, :].rearrange("(i m) w -> i m w", m=4), in_=ot[:])
+
+        stats(0)
+        for b in range(B):
+            if b + 1 < B:
+                stats(b + 1)
+            tq = topq.tile([P, 2, D], U32, name="tq", align_bytes=64)
+            ts = topq.tile([P, 2, D], U8, name="ts", align_bytes=64)
+            prep_top(b, 1, "v", tq, ts)
+            prep_top(b, 0, "v", tq, ts)
+            for n in range(N):
+                cq = gq.tile([P, 2, D], U32, name="cq", align_bytes=64)
+                cs = gq.tile([P, 2, D], U8, name="cs", align_bytes=64)
+                prep_g(b, n, 1, "v", cq, cs)
+                cast(b, n)
+                prep_g(b, n, 0, "s", cq, cs)
+                flush()
+                mm(b, n, tq, ts, cq, cs)

@@ -27,127 +27,162 @@ FLT_MAX = 3.4028234663852886e38
 def tile_updateonrightwithselectiveresetonleft_kernel(tc, A1_atop_B1, A2_atop_B2, grad_out, out):
     nc = tc.nc
     with ExitStack() as ctx:
+        ctx.enter_context(tc.manual_schedule())
         const = ctx.enter_context(tc.tile_pool(name="const", bufs=1))
         rawp = ctx.enter_context(tc.tile_pool(name="raw", bufs=1))
-        scrp = ctx.enter_context(tc.tile_pool(name="scr", bufs=3))
+        scrp = ctx.enter_context(tc.tile_pool(name="scr", bufs=2))
         small = ctx.enter_context(tc.tile_pool(name="small", bufs=2))
-        grpp = ctx.enter_context(tc.tile_pool(name="grp", bufs=5))
+        grpp = ctx.enter_context(tc.tile_pool(name="grp", bufs=4))
+        grps = ctx.enter_context(tc.tile_pool(name="grps", bufs=2))
         topq = ctx.enter_context(tc.tile_pool(name="topq", bufs=2))
         gq = ctx.enter_context(tc.tile_pool(name="gq", bufs=3))
         outp = ctx.enter_context(tc.tile_pool(name="outp", bufs=8))
-        accp = ctx.enter_context(tc.psum_pool(name="accp", bufs=6))
-        pstat = ctx.enter_context(tc.psum_pool(name="pstat", bufs=2))
+        accp = ctx.enter_context(tc.psum_pool(name="accp", bufs=7))
+        pstat = ctx.enter_context(tc.psum_pool(name="pstat", bufs=1))
 
-        raw_top = []
-        raw_g = []
-        for b in range(B):
-            rt = rawp.tile([P, 2, 4, D], BF16, name="rt%d" % b)
-            raw_top.append(rt)
-            for c in range(2):
-                nc.sync.dma_start(
-                    out=rt[:, c],
-                    in_=A1_atop_B1[b, 0, c * D:(c + 1) * D, :].rearrange("(p j) w -> p j w", j=4),
-                )
-            row = []
-            for n in range(N):
-                rg = rawp.tile([P, 2, 4, D], BF16, name="rg%d%d" % (b, n))
-                row.append(rg)
-                for c in (1, 0):
-                    nc.sync.dma_start(
-                        out=rg[:, c],
-                        in_=grad_out[b, n, c * D:(c + 1) * D, :].rearrange("(p j) w -> p j w", j=4),
-                    )
-            raw_g.append(row)
+        raw_top = [rawp.tile([P, 2, 4, D], BF16, name="rt%d" % b) for b in range(B)]
+        raw_g = [[rawp.tile([P, 2, 4, D], BF16, name="rg%d%d" % (b, n)) for n in range(N)] for b in range(B)]
+
+        def load_top(b, c):
+            nc.sync.dma_start(out=raw_top[b][:, c],
+                              in_=A1_atop_B1[b, 0, c * D:(c + 1) * D, :].rearrange("(p j) w -> p j w", j=4))
+
+        def load_g(b, n, c):
+            nc.sync.dma_start(out=raw_g[b][n][:, c],
+                              in_=grad_out[b, n, c * D:(c + 1) * D, :].rearrange("(p j) w -> p j w", j=4))
+
+        load_top(0, 0)
+        load_top(0, 1)
+        load_g(0, 0, 1)
+        load_g(0, 0, 0)
+        load_top(1, 0)
+        load_g(0, 1, 0)
+        load_top(1, 1)
+        load_g(0, 1, 1)
+        load_top(2, 0)
+        load_top(2, 1)
+        load_g(1, 0, 1)
+        load_g(1, 0, 0)
+        load_g(1, 1, 0)
+        load_g(1, 1, 1)
+        load_top(3, 0)
+        load_top(3, 1)
+        for b in (2, 3):
+            load_g(b, 0, 1)
+            load_g(b, 0, 0)
+            load_g(b, 1, 0)
+            load_g(b, 1, 1)
 
         ident = const.tile([P, P], F32, name="ident")
         make_identity(nc, ident[:])
+        junk = const.tile([P, W], BF16, name="junk")
 
-        factor = {}
+        st = {}
+        tl = {}
 
-        def stats(b):
-            rt = raw_top[b]
-            abs_a = scrp.tile([P, W], BF16, name="abs_a", tag="scr")
-            sum_a = small.tile([P, 1], F32, name="sum_a")
-            nc.scalar.activation(out=abs_a[:], in_=rt[:, 0].rearrange("p j w -> p (j w)"), func=ACT.Abs,
-                                 accum_out=sum_a[:])
-            vstat = small.tile([P, 2], F32, name="vstat")
-            junk = scrp.tile([P, W], BF16, name="junk", tag="scr")
-            nc.vector.tensor_scalar(out=junk[:], in0=rt[:, 1].rearrange("p j w -> p (j w)"), scalar1=0.0,
-                                    scalar2=None, op0=ALU.not_equal, op1=ALU.max, accum_out=vstat[:, 1:2])
-            nc.vector.tensor_scalar(out=abs_a[:], in0=abs_a[:], scalar1=1.0, scalar2=None, op0=ALU.mult,
-                                    op1=ALU.max, accum_out=vstat[:, 0:1])
+        def s_abs(b):
+            st["abs", b] = scrp.tile([P, W], BF16, name="abs_a")
+            st["sum", b] = small.tile([P, 1], F32, name="sum_a")
+            nc.scalar.activation(out=st["abs", b][:], in_=raw_top[b][:, 0].rearrange("p j w -> p (j w)"),
+                                 func=ACT.Abs, accum_out=st["sum", b][:])
+
+        def v_nz(b):
+            st["vs", b] = small.tile([P, 2], F32, name="vstat")
+            nc.vector.tensor_scalar(out=junk[:], in0=raw_top[b][:, 1].rearrange("p j w -> p (j w)"), scalar1=0.0,
+                                    scalar2=None, op0=ALU.not_equal, op1=ALU.max, accum_out=st["vs", b][:, 1:2])
+
+        def v_mx(b):
+            a = st["abs", b]
+            nc.vector.tensor_scalar(out=a[:], in0=a[:], scalar1=1.0, scalar2=None, op0=ALU.mult,
+                                    op1=ALU.max, accum_out=st["vs", b][:, 0:1])
+
+        def pe_tr(b):
             ps = pstat.tile([P, 3, P], F32, name="ps")
-            nc.tensor.transpose(out=ps[:, 0, :], in_=vstat[:, 0:1].to_broadcast([P, P]), identity=ident[:])
-            nc.tensor.transpose(out=ps[:, 1, :], in_=vstat[:, 1:2].to_broadcast([P, P]), identity=ident[:])
-            nc.tensor.transpose(out=ps[:, 2, :], in_=sum_a[:, 0:1].to_broadcast([P, P]), identity=ident[:])
-            red = small.tile([P, 2], F32, name="red")
-            nc.vector.tensor_reduce(out=red[:], in_=ps[:, 0:2, :], axis=AX.X, op=ALU.max)
-            tot = small.tile([P, 1], F32, name="tot")
-            nc.vector.tensor_reduce(out=tot[:], in_=ps[:, 2, :], axis=AX.X, op=ALU.add)
-            u = small.tile([P, 1], F32, name="u")
-            nc.vector.tensor_scalar(out=u[:], in0=red[:, 1:2], scalar1=0.0, scalar2=tot[:, 0:1],
-                                    op0=ALU.is_equal, op1=ALU.mult)
-            h = small.tile([P, 1], F32, name="h")
-            nc.vector.tensor_scalar(out=h[:], in0=u[:], scalar1=float(D * D), scalar2=FLT_MAX,
+            st["ps", b] = ps
+            vs = st["vs", b]
+            nc.tensor.transpose(out=ps[:, 0, :], in_=vs[:, 0:1].to_broadcast([P, P]), identity=ident[:])
+            nc.tensor.transpose(out=ps[:, 1, :], in_=vs[:, 1:2].to_broadcast([P, P]), identity=ident[:])
+            nc.tensor.transpose(out=ps[:, 2, :], in_=st["sum", b][:, 0:1].to_broadcast([P, P]), identity=ident[:])
+
+        def v_red(b):
+            ps = st["ps", b]
+            st["red", b] = small.tile([P, 2], F32, name="red")
+            nc.vector.tensor_reduce(out=st["red", b][:], in_=ps[:, 0:2, :], axis=AX.X, op=ALU.max)
+            st["tot", b] = small.tile([P, 1], F32, name="tot")
+            nc.vector.tensor_reduce(out=st["tot", b][:], in_=ps[:, 2, :], axis=AX.X, op=ALU.add)
+
+        def v_u(b):
+            st["u", b] = small.tile([P, 1], F32, name="u")
+            nc.vector.tensor_scalar(out=st["u", b][:], in0=st["red", b][:, 1:2], scalar1=0.0,
+                                    scalar2=st["tot", b][:, 0:1], op0=ALU.is_equal, op1=ALU.mult)
+
+        def v_hg(b):
+            st["h", b] = small.tile([P, 1], F32, name="h")
+            nc.vector.tensor_scalar(out=st["h", b][:], in0=st["u", b][:], scalar1=float(D * D), scalar2=FLT_MAX,
                                     op0=ALU.is_gt, op1=ALU.mult)
-            g = small.tile([P, 1], F32, name="g")
-            nc.vector.tensor_scalar(out=g[:], in0=u[:], scalar1=float(D * D), scalar2=None, op0=ALU.is_le)
-            den = small.tile([P, 1], F32, name="den")
-            nc.vector.scalar_tensor_tensor(out=den[:], in0=red[:, 0:1], scalar=h[:, 0:1], in1=g[:],
-                                           op0=ALU.min, op1=ALU.max)
-            f = small.tile([P, 1], F32, name="f")
-            nc.vector.reciprocal(out=f[:], in_=den[:])
-            factor[b] = f
+            st["g", b] = small.tile([P, 1], F32, name="g")
+            nc.vector.tensor_scalar(out=st["g", b][:], in0=st["u", b][:], scalar1=float(D * D), scalar2=None,
+                                    op0=ALU.is_le)
 
-        pending = []
+        def v_den(b):
+            st["den", b] = small.tile([P, 1], F32, name="den")
+            nc.vector.scalar_tensor_tensor(out=st["den", b][:], in0=st["red", b][:, 0:1], scalar=st["h", b][:, 0:1],
+                                           in1=st["g", b][:], op0=ALU.min, op1=ALU.max)
 
-        def flush():
-            while pending:
-                pending.pop(0)()
+        def v_f(b):
+            st["f", b] = small.tile([P, 1], F32, name="f")
+            nc.vector.reciprocal(out=st["f", b][:], in_=st["den", b][:])
 
-        def unit(eng, src, dst_view, src_view, grp, codes, scales, fmt, scale=None):
-            if eng == "v":
-                if scale is None:
-                    nc.vector.tensor_copy(out=dst_view, in_=src_view)
-                else:
-                    nc.vector.tensor_scalar(out=dst_view, in0=src_view, scalar1=scale, scalar2=None, op0=ALU.mult)
-            else:
-                if scale is None:
-                    nc.scalar.copy(out=dst_view, in_=src_view)
-                else:
-                    nc.scalar.activation(out=dst_view, in_=src_view, func=ACT.Copy, scale=scale)
-            flush()
-
-            def quant():
-                nc.vector.quantize_mx(out=codes.bitcast(fmt), scales=scales, in_=grp)
-            pending.append(quant)
-
-        def prep_top(b, c, eng, tq, ts):
+        def rg_top(b, c):
             grp = grpp.tile([P, 4, P, 4], BF16, name="grp_t", tag="grp", align_bytes=64)
-            unit(eng, None,
-                 grp[:].rearrange("p m i j -> p i j m"),
-                 raw_top[b][:, c].rearrange("p j (i m) -> p i j m", m=4),
-                 grp[:].rearrange("p m i j -> p (m i j)"),
-                 tq[:, c, :], ts[:, c, :], E4,
-                 scale=(factor[b][:, 0:1] if c == 0 else None))
+            tl["gt", b, c] = grp
+            dst = grp[:].rearrange("p m i j -> p i j m")
+            src = raw_top[b][:, c].rearrange("p j (i m) -> p i j m", m=4)
+            if c == 0:
+                nc.vector.tensor_scalar(out=dst, in0=src, scalar1=st["f", b][:, 0:1], scalar2=None, op0=ALU.mult)
+            else:
+                nc.vector.tensor_copy(out=dst, in_=src)
 
-        def prep_g(b, n, c, eng, cq, cs):
-            grp = grpp.tile([P, D, 4], BF16, name="grp_g", tag="grp", align_bytes=64)
-            unit(eng, None,
-                 grp[:].rearrange("p (c i) t -> p c t i", i=4),
-                 raw_g[b][n][:, c].rearrange("p t (c i) -> p c t i", i=4),
-                 grp[:].rearrange("p w t -> p (w t)"),
-                 cq[:, c, :], cs[:, c, :], E5)
+        def q_top(b, c):
+            if ("tq", b) not in tl:
+                tl["tq", b] = topq.tile([P, 2, D], U32, name="tq", align_bytes=64)
+                tl["ts", b] = topq.tile([P, 2, D], U8, name="ts", align_bytes=64)
+            nc.vector.quantize_mx(out=tl["tq", b][:, c, :].bitcast(E4), scales=tl["ts", b][:, c, :],
+                                  in_=tl["gt", b, c][:].rearrange("p m i j -> p (m i j)"))
 
-        def cast(b, n):
+        def rg_g(b, n, c, eng):
+            if eng == "v":
+                grp = grpp.tile([P, D, 4], BF16, name="grp_g", tag="grp", align_bytes=64)
+            else:
+                grp = grps.tile([P, D, 4], BF16, name="grp_s", align_bytes=64)
+            tl["gg", b, n, c] = grp
+            dst = grp[:].rearrange("p (c i) t -> p c t i", i=4)
+            src = raw_g[b][n][:, c].rearrange("p t (c i) -> p c t i", i=4)
+            if eng == "v":
+                nc.vector.tensor_copy(out=dst, in_=src)
+            else:
+                nc.scalar.copy(out=dst, in_=src)
+
+        def q_g(b, n, c):
+            if ("cq", b, n) not in tl:
+                tl["cq", b, n] = gq.tile([P, 2, D], U32, name="cq", align_bytes=64)
+                tl["cs", b, n] = gq.tile([P, 2, D], U8, name="cs", align_bytes=64)
+            nc.vector.quantize_mx(out=tl["cq", b, n][:, c, :].bitcast(E5), scales=tl["cs", b, n][:, c, :],
+                                  in_=tl["gg", b, n, c][:].rearrange("p w t -> p (w t)"))
+
+        def cast(b, n, eng):
             ot = outp.tile([P, 4, D], F32, name="ot_c", tag="ot")
-            nc.vector.tensor_copy(out=ot[:], in_=raw_g[b][n][:, 1])
+            if eng == "v":
+                nc.vector.tensor_copy(out=ot[:], in_=raw_g[b][n][:, 1])
+            else:
+                nc.scalar.copy(out=ot[:], in_=raw_g[b][n][:, 1])
             nc.sync.dma_start(out=out[b, n, D:2 * D, :].rearrange("(p j) w -> p j w", j=4), in_=ot[:])
 
-        def mm(b, n, tq, ts, cq, cs):
-            ot = outp.tile([P, 4, D], F32, name="ot_m", tag="ot")
-            for m in range(4):
+        def mm(b, n, order):
+            tq, ts, cq, cs = tl["tq", b], tl["ts", b], tl["cq", b, n], tl["cs", b, n]
+            for m in order:
                 acc = accp.tile([P, D], F32, name="acc")
+                tl["acc", b, n, m] = acc
                 for k, c in enumerate((1, 0)):
                     nc.tensor.matmul_mx(
                         out=acc[:],
@@ -158,22 +193,90 @@ def tile_updateonrightwithselectiveresetonleft_kernel(tc, A1_atop_B1, A2_atop_B2
                         start=(k == 0),
                         stop=(k == 1),
                     )
-                nc.scalar.copy(out=ot[:, m, :], in_=acc[:])
+
+        def evac(b, n):
+            ot = outp.tile([P, 4, D], F32, name="ot_m", tag="ot")
+            for m in range(4):
+                nc.scalar.copy(out=ot[:, m, :], in_=tl["acc", b, n, m][:])
             nc.sync.dma_start(out=out[b, n, 0:D, :].rearrange("(i m) w -> i m w", m=4), in_=ot[:])
 
-        stats(0)
-        for b in range(B):
-            if b + 1 < B:
-                stats(b + 1)
-            tq = topq.tile([P, 2, D], U32, name="tq", align_bytes=64)
-            ts = topq.tile([P, 2, D], U8, name="ts", align_bytes=64)
-            prep_top(b, 1, "v", tq, ts)
-            prep_top(b, 0, "v", tq, ts)
-            for n in range(N):
-                cq = gq.tile([P, 2, D], U32, name="cq", align_bytes=64)
-                cs = gq.tile([P, 2, D], U8, name="cs", align_bytes=64)
-                prep_g(b, n, 1, "v", cq, cs)
-                cast(b, n)
-                prep_g(b, n, 0, "s", cq, cs)
-                flush()
-                mm(b, n, tq, ts, cq, cs)
+        def evac_last(b, n):
+            dst = out[b, n, 0:D, :].rearrange("(i m) w -> i m w", m=4)
+            o_s = outp.tile([P, 2, D], F32, name="ot_s", tag="ot")
+            o_v = outp.tile([P, 2, D], F32, name="ot_v", tag="ot")
+            nc.scalar.copy(out=o_s[:, 0, :], in_=tl["acc", b, n, 0][:])
+            nc.vector.tensor_copy(out=o_v[:, 0, :], in_=tl["acc", b, n, 2][:])
+            nc.scalar.copy(out=o_s[:, 1, :], in_=tl["acc", b, n, 1][:])
+            nc.vector.tensor_copy(out=o_v[:, 1, :], in_=tl["acc", b, n, 3][:])
+            nc.sync.dma_start(out=dst[:, 0:2, :], in_=o_s[:])
+            nc.sync.dma_start(out=dst[:, 2:4, :], in_=o_v[:])
+
+        s_abs(0)
+        v_nz(0)
+        v_mx(0)
+        pe_tr(0)
+        cast(0, 0, "s")
+        s_abs(1)
+        rg_top(0, 1)
+        v_red(0)
+        rg_g(0, 0, 1, "v")
+        v_u(0)
+        q_top(0, 1)
+        v_hg(0)
+        rg_g(0, 0, 0, "v")
+        v_den(0)
+        q_g(0, 0, 1)
+        v_f(0)
+        q_g(0, 0, 0)
+        rg_top(0, 0)
+        v_nz(1)
+        q_top(0, 0)
+        v_mx(1)
+        rg_g(0, 1, 0, "s")
+        pe_tr(1)
+        mm(0, 0, (0, 1, 2, 3))
+
+        for s in range(1, 2 * B):
+            b, n = s // 2, s % 2
+            pb, pn = (s - 1) // 2, (s - 1) % 2
+            last_b = b == B - 1
+            if n == 0:
+                if not last_b:
+                    rg_g(b, 1, 0, "s")
+                cast(b, 0, "s")
+                evac(pb, pn)
+                rg_g(b, 0, 1, "v")
+                rg_top(b, 0)
+                q_g(b, 0, 1)
+                if not last_b:
+                    v_nz(b + 1)
+                q_top(b, 0)
+                rg_g(b, 0, 0, "v")
+                if not last_b:
+                    v_mx(b + 1)
+                else:
+                    rg_g(b, 1, 0, "v")
+                q_g(b, 0, 0)
+                if not last_b:
+                    pe_tr(b + 1)
+                mm(b, 0, (0, 1, 2, 3))
+            else:
+                if b + 2 < B:
+                    s_abs(b + 2)
+                cast(b, 1, "s")
+                evac(pb, pn)
+                rg_g(b, 1, 1, "v")
+                if not last_b:
+                    v_red(b + 1)
+                    rg_top(b + 1, 1)
+                    v_u(b + 1)
+                q_g(b, 1, 0)
+                if not last_b:
+                    v_hg(b + 1)
+                q_g(b, 1, 1)
+                mm(b, 1, (0, 2, 1, 3) if last_b else (0, 1, 2, 3))
+                if not last_b:
+                    v_den(b + 1)
+                    q_top(b + 1, 1)
+                    v_f(b + 1)
+        evac_last(B - 1, 1)

@@ -51,6 +51,14 @@ def tile_updateonrightwithselectiveresetonleft_kernel(tc, A1_atop_B1, A2_atop_B2
             nc.sync.dma_start(out=raw_g[b][n][:, c],
                               in_=grad_out[b, n, c * D:(c + 1) * D, :].rearrange("(p j) w -> p j w", j=4))
 
+        def load_top_whole(b):
+            nc.sync.dma_start(out=raw_top[b][:],
+                              in_=A1_atop_B1[b, 0].rearrange("(c p j) w -> p c j w", c=2, j=4))
+
+        def load_g_whole(b, n):
+            nc.sync.dma_start(out=raw_g[b][n][:],
+                              in_=grad_out[b, n].rearrange("(c p j) w -> p c j w", c=2, j=4))
+
         load_top(0, 0)
         load_top(0, 1)
         load_g(0, 0, 1)
@@ -59,19 +67,13 @@ def tile_updateonrightwithselectiveresetonleft_kernel(tc, A1_atop_B1, A2_atop_B2
         load_g(0, 1, 0)
         load_top(1, 1)
         load_g(0, 1, 1)
-        load_top(2, 0)
-        load_top(2, 1)
-        load_g(1, 0, 1)
-        load_g(1, 0, 0)
-        load_g(1, 1, 0)
-        load_g(1, 1, 1)
-        load_top(3, 0)
-        load_top(3, 1)
+        load_top_whole(2)
+        load_g_whole(1, 0)
+        load_g_whole(1, 1)
+        load_top_whole(3)
         for b in (2, 3):
-            load_g(b, 0, 1)
-            load_g(b, 0, 0)
-            load_g(b, 1, 0)
-            load_g(b, 1, 1)
+            load_g_whole(b, 0)
+            load_g_whole(b, 1)
 
         ident = const.tile([P, P], F32, name="ident")
         make_identity(nc, ident[:])

@@ -37,7 +37,8 @@ def tile_updateonrightwithselectiveresetonleft_kernel(tc, A1_atop_B1, A2_atop_B2
         topq = ctx.enter_context(tc.tile_pool(name="topq", bufs=2))
         gq = ctx.enter_context(tc.tile_pool(name="gq", bufs=3))
         outp = ctx.enter_context(tc.tile_pool(name="outp", bufs=8))
-        accp = ctx.enter_context(tc.psum_pool(name="accp", bufs=7))
+        accp = ctx.enter_context(tc.psum_pool(name="accp", bufs=5))
+        rgp = ctx.enter_context(tc.psum_pool(name="rgp", bufs=2))
         pstat = ctx.enter_context(tc.psum_pool(name="pstat", bufs=1))
 
         raw_top = [rawp.tile([P, 2, 4, D], BF16, name="rt%d" % b) for b in range(B)]
@@ -77,6 +78,8 @@ def tile_updateonrightwithselectiveresetonleft_kernel(tc, A1_atop_B1, A2_atop_B2
 
         ident = const.tile([P, P], F32, name="ident")
         make_identity(nc, ident[:])
+        ident_bf = const.tile([P, P], BF16, name="ident_bf")
+        make_identity(nc, ident_bf[:])
         junk = const.tile([P, W], BF16, name="junk")
 
         st = {}
@@ -165,6 +168,23 @@ def tile_updateonrightwithselectiveresetonleft_kernel(tc, A1_atop_B1, A2_atop_B2
             else:
                 nc.scalar.copy(out=dst, in_=src)
 
+        def pe_rg(b, n, c):
+            for h in range(2):
+                ps = rgp.tile([P, 2, P, 4], BF16, name="ps_rg")
+                tl["pr", b, n, c, h] = ps
+                for q in range(2):
+                    w0 = (2 * h + q) * P
+                    nc.tensor.matmul(out=ps[:, q], lhsT=ident_bf[:],
+                                     rhs=raw_g[b][n][:, c, :, w0:w0 + P].rearrange("p t w -> p w t"),
+                                     start=True, stop=True)
+
+        def s_rg(b, n, c):
+            grp = grps.tile([P, D, 4], BF16, name="grp_s", align_bytes=64)
+            tl["gg", b, n, c] = grp
+            for h in range(2):
+                nc.scalar.copy(out=grp[:, h * 2 * P:(h + 1) * 2 * P, :],
+                               in_=tl["pr", b, n, c, h][:].rearrange("p q w t -> p (q w) t"))
+
         def q_g(b, n, c):
             if ("cq", b, n) not in tl:
                 tl["cq", b, n] = gq.tile([P, 2, D], U32, name="cq", align_bytes=64)
@@ -243,8 +263,7 @@ def tile_updateonrightwithselectiveresetonleft_kernel(tc, A1_atop_B1, A2_atop_B2
             pb, pn = (s - 1) // 2, (s - 1) % 2
             last_b = b == B - 1
             if n == 0:
-                if not last_b:
-                    rg_g(b, 1, 0, "s")
+                s_rg(b, 0, 0)
                 cast(b, 0, "s")
                 evac(pb, pn)
                 rg_g(b, 0, 1, "v")
@@ -253,19 +272,20 @@ def tile_updateonrightwithselectiveresetonleft_kernel(tc, A1_atop_B1, A2_atop_B2
                 if not last_b:
                     v_nz(b + 1)
                 q_top(b, 0)
-                rg_g(b, 0, 0, "v")
                 if not last_b:
                     v_mx(b + 1)
-                else:
-                    rg_g(b, 1, 0, "v")
                 q_g(b, 0, 0)
+                pe_rg(b, 1, 0)
                 if not last_b:
                     pe_tr(b + 1)
                 mm(b, 0, (0, 1, 2, 3))
             else:
+                if b > 0:
+                    s_rg(b, 1, 0)
                 if b + 2 < B:
                     s_abs(b + 2)
-                cast(b, 1, "s")
+                if not last_b:
+                    cast(b, 1, "s")
                 evac(pb, pn)
                 rg_g(b, 1, 1, "v")
                 if not last_b:
@@ -276,9 +296,13 @@ def tile_updateonrightwithselectiveresetonleft_kernel(tc, A1_atop_B1, A2_atop_B2
                 if not last_b:
                     v_hg(b + 1)
                 q_g(b, 1, 1)
+                if not last_b:
+                    pe_rg(b + 1, 0, 0)
                 mm(b, 1, (0, 2, 1, 3) if last_b else (0, 1, 2, 3))
                 if not last_b:
                     v_den(b + 1)
                     q_top(b + 1, 1)
                     v_f(b + 1)
+                else:
+                    cast(b, 1, "v")
         evac_last(B - 1, 1)

@@ -198,7 +198,10 @@ def tile_updateonrightwithselectiveresetonleft_kernel(tc, A1_atop_B1, A2_atop_B2
                 nc.vector.tensor_copy(out=ot[:], in_=raw_g[b][n][:, 1])
             else:
                 nc.scalar.copy(out=ot[:], in_=raw_g[b][n][:, 1])
-            nc.sync.dma_start(out=out[b, n, D:2 * D, :].rearrange("(p j) w -> p j w", j=4), in_=ot[:])
+            tl["oc", b, n] = ot
+
+        def cast_store(b, n, queue):
+            queue.dma_start(out=out[b, n, D:2 * D, :].rearrange("(p j) w -> p j w", j=4), in_=tl["oc", b, n][:])
 
         def mm(b, n, order):
             tq, ts, cq, cs = tl["tq", b], tl["ts", b], tl["cq", b, n], tl["cs", b, n]
@@ -230,7 +233,7 @@ def tile_updateonrightwithselectiveresetonleft_kernel(tc, A1_atop_B1, A2_atop_B2
             nc.vector.tensor_copy(out=o_v[:, 0, :], in_=tl["acc", b, n, 2][:])
             nc.scalar.copy(out=o_s[:, 1, :], in_=tl["acc", b, n, 1][:])
             nc.vector.tensor_copy(out=o_v[:, 1, :], in_=tl["acc", b, n, 3][:])
-            nc.sync.dma_start(out=dst[:, 0:2, :], in_=o_s[:])
+            nc.scalar.dma_start(out=dst[:, 0:2, :], in_=o_s[:])
             nc.sync.dma_start(out=dst[:, 2:4, :], in_=o_v[:])
 
         s_abs(0)
@@ -238,6 +241,7 @@ def tile_updateonrightwithselectiveresetonleft_kernel(tc, A1_atop_B1, A2_atop_B2
         v_mx(0)
         pe_tr(0)
         cast(0, 0, "s")
+        cast_store(0, 0, nc.sync)
         s_abs(1)
         rg_top(0, 1)
         v_red(0)
@@ -265,7 +269,11 @@ def tile_updateonrightwithselectiveresetonleft_kernel(tc, A1_atop_B1, A2_atop_B2
             if n == 0:
                 s_rg(b, 0, 0)
                 cast(b, 0, "s")
+                if s < 3:
+                    cast_store(b, 0, nc.sync)
                 evac(pb, pn)
+                if s >= 3:
+                    cast_store(b, 0, nc.scalar)
                 rg_g(b, 0, 1, "v")
                 rg_top(b, 0)
                 q_g(b, 0, 1)
@@ -286,7 +294,11 @@ def tile_updateonrightwithselectiveresetonleft_kernel(tc, A1_atop_B1, A2_atop_B2
                     s_abs(b + 2)
                 if not last_b:
                     cast(b, 1, "s")
+                    if s < 3:
+                        cast_store(b, 1, nc.sync)
                 evac(pb, pn)
+                if s >= 3 and not last_b:
+                    cast_store(b, 1, nc.scalar)
                 rg_g(b, 1, 1, "v")
                 if not last_b:
                     v_red(b + 1)
@@ -305,4 +317,5 @@ def tile_updateonrightwithselectiveresetonleft_kernel(tc, A1_atop_B1, A2_atop_B2
                     v_f(b + 1)
                 else:
                     cast(b, 1, "v")
+                    cast_store(b, 1, nc.scalar)
         evac_last(B - 1, 1)

@@ -41,8 +41,8 @@ def tile_updateonrightwithselectiveresetonleft_kernel(tc, A1_atop_B1, A2_atop_B2
         rgp = ctx.enter_context(tc.psum_pool(name="rgp", bufs=2))
         pstat = ctx.enter_context(tc.psum_pool(name="pstat", bufs=1))
 
-        raw_top = [rawp.tile([P, 2, 4, D], BF16, name="rt%d" % b) for b in range(B)]
-        raw_g = [[rawp.tile([P, 2, 4, D], BF16, name="rg%d%d" % (b, n)) for n in range(N)] for b in range(B)]
+        raw_top = [rawp.tile([P, 2, 4, D], BF16, name="rt%d" % b, align_bytes=256) for b in range(B)]
+        raw_g = [[rawp.tile([P, 2, 4, D], BF16, name="rg%d%d" % (b, n), align_bytes=256) for n in range(N)] for b in range(B)]
 
         def load_top(b, c):
             nc.sync.dma_start(out=raw_top[b][:, c],
@@ -193,7 +193,7 @@ def tile_updateonrightwithselectiveresetonleft_kernel(tc, A1_atop_B1, A2_atop_B2
                                   in_=tl["gg", b, n, c][:].rearrange("p w t -> p (w t)"))
 
         def cast(b, n, eng):
-            ot = outp.tile([P, 4, D], F32, name="ot_c", tag="ot")
+            ot = outp.tile([P, 4, D], F32, name="ot_c", tag="ot", align_bytes=256)
             if eng == "v":
                 nc.vector.tensor_copy(out=ot[:], in_=raw_g[b][n][:, 1])
             else:
@@ -220,15 +220,15 @@ def tile_updateonrightwithselectiveresetonleft_kernel(tc, A1_atop_B1, A2_atop_B2
                     )
 
         def evac(b, n):
-            ot = outp.tile([P, 4, D], F32, name="ot_m", tag="ot")
+            ot = outp.tile([P, 4, D], F32, name="ot_m", tag="ot", align_bytes=256)
             for m in range(4):
                 nc.scalar.copy(out=ot[:, m, :], in_=tl["acc", b, n, m][:])
             nc.sync.dma_start(out=out[b, n, 0:D, :].rearrange("(i m) w -> i m w", m=4), in_=ot[:])
 
         def evac_last(b, n):
             dst = out[b, n, 0:D, :].rearrange("(i m) w -> i m w", m=4)
-            o_s = outp.tile([P, 2, D], F32, name="ot_s", tag="ot")
-            o_v = outp.tile([P, 2, D], F32, name="ot_v", tag="ot")
+            o_s = outp.tile([P, 2, D], F32, name="ot_s", tag="ot", align_bytes=256)
+            o_v = outp.tile([P, 2, D], F32, name="ot_v", tag="ot", align_bytes=256)
             nc.scalar.copy(out=o_s[:, 0, :], in_=tl["acc", b, n, 0][:])
             nc.vector.tensor_copy(out=o_v[:, 0, :], in_=tl["acc", b, n, 2][:])
             nc.scalar.copy(out=o_s[:, 1, :], in_=tl["acc", b, n, 1][:])

@@ -68,13 +68,6 @@ def tile_updateonrightwithselectiveresetonleft_kernel(tc, A1_atop_B1, A2_atop_B2
         load_g(0, 1, 0)
         load_top(1, 1)
         load_g(0, 1, 1)
-        load_top_whole(2)
-        load_g_whole(1, 0)
-        load_g_whole(1, 1)
-        load_top_whole(3)
-        for b in (2, 3):
-            load_g_whole(b, 0)
-            load_g_whole(b, 1)
 
         ident = const.tile([P, P], F32, name="ident")
         make_identity(nc, ident[:])
@@ -241,8 +234,12 @@ def tile_updateonrightwithselectiveresetonleft_kernel(tc, A1_atop_B1, A2_atop_B2
         v_mx(0)
         pe_tr(0)
         cast(0, 0, "s")
-        cast_store(0, 0, nc.sync)
         s_abs(1)
+        cast_store(0, 0, nc.scalar)
+        load_top_whole(2)
+        load_g_whole(1, 0)
+        load_g_whole(1, 1)
+        load_g_whole(2, 0)
         rg_top(0, 1)
         v_red(0)
         rg_g(0, 0, 1, "v")
@@ -269,11 +266,8 @@ def tile_updateonrightwithselectiveresetonleft_kernel(tc, A1_atop_B1, A2_atop_B2
             if n == 0:
                 s_rg(b, 0, 0)
                 cast(b, 0, "s")
-                if s < 3:
-                    cast_store(b, 0, nc.sync)
                 evac(pb, pn)
-                if s >= 3:
-                    cast_store(b, 0, nc.scalar)
+                cast_store(b, 0, nc.scalar)
                 rg_g(b, 0, 1, "v")
                 rg_top(b, 0)
                 q_g(b, 0, 1)
@@ -294,10 +288,14 @@ def tile_updateonrightwithselectiveresetonleft_kernel(tc, A1_atop_B1, A2_atop_B2
                     s_abs(b + 2)
                 if not last_b:
                     cast(b, 1, "s")
-                    if s < 3:
-                        cast_store(b, 1, nc.sync)
+                if s == 1:
+                    cast_store(0, 1, nc.scalar)
+                    load_top_whole(3)
+                    load_g_whole(2, 1)
+                    load_g_whole(3, 0)
+                    load_g_whole(3, 1)
                 evac(pb, pn)
-                if s >= 3 and not last_b:
+                if 1 < s and not last_b:
                     cast_store(b, 1, nc.scalar)
                 rg_g(b, 1, 1, "v")
                 if not last_b:

@@ -292,9 +292,10 @@ def tile_updateonrightwithselectiveresetonleft_kernel(tc, A1_atop_B1, A2_atop_B2
                     cast_store(0, 1, nc.scalar)
                     load_top_whole(3)
                     load_g_whole(2, 1)
+                evac(pb, pn)
+                if s == 1:
                     load_g_whole(3, 0)
                     load_g_whole(3, 1)
-                evac(pb, pn)
                 if 1 < s and not last_b:
                     cast_store(b, 1, nc.scalar)
                 rg_g(b, 1, 1, "v")

from contextlib import ExitStack

import concourse.mybir as mybir
from concourse.masks import make_identity

FLOPS = 2 * 4 * 2 * 512 * 1024 * 512
BYTES = 4 * 1024 * 512 * 2 + 8 * 1024 * 512 * 2 + 8 * 1024 * 512 * 4

BF16 = mybir.dt.bfloat16
F32 = mybir.dt.float32
U32 = mybir.dt.uint32
U8 = mybir.dt.uint8
E4 = mybir.dt.float8_e4m3fn_x4
E5 = mybir.dt.float8_e5m2_x4
ALU = mybir.AluOpType
ACT = mybir.ActivationFunctionType
AX = mybir.AxisListType

P = 128
D = 512
B = 4
N = 2
W = 4 * D
FLT_MAX = 3.4028234663852886e38


def tile_updateonrightwithselectiveresetonleft_kernel(tc, A1_atop_B1, A2_atop_B2, grad_out, out):
    nc = tc.nc
    with ExitStack() as ctx:
        ctx.enter_context(tc.manual_schedule())
        const = ctx.enter_context(tc.tile_pool(name="const", bufs=1))
        rawp = ctx.enter_context(tc.tile_pool(name="raw", bufs=1))
        scrp = ctx.enter_context(tc.tile_pool(name="scr", bufs=2))
        small = ctx.enter_context(tc.tile_pool(name="small", bufs=2))
        grpp = ctx.enter_context(tc.tile_pool(name="grp", bufs=4))
        grps = ctx.enter_context(tc.tile_pool(name="grps", bufs=2))
        topq = ctx.enter_context(tc.tile_pool(name="topq", bufs=2))
        gq = ctx.enter_context(tc.tile_pool(name="gq", bufs=3))
        outp = ctx.enter_context(tc.tile_pool(name="outp", bufs=8))
        accp = ctx.enter_context(tc.psum_pool(name="accp", bufs=5))
        rgp = ctx.enter_context(tc.psum_pool(name="rgp", bufs=2))
        pstat = ctx.enter_context(tc.psum_pool(name="pstat", bufs=1))

        raw_top = [rawp.tile([P, 2, 4, D], BF16, name="rt%d" % b, align_bytes=256) for b in range(B)]
        raw_g = [[rawp.tile([P, 2, 4, D], BF16, name="rg%d%d" % (b, n), align_bytes=256) for n in range(N)] for b in range(B)]

        def load_top(b, c):
            nc.sync.dma_start(out=raw_top[b][:, c],
                              in_=A1_atop_B1[b, 0, c * D:(c + 1) * D, :].rearrange("(p j) w -> p j w", j=4))

        def load_g(b, n, c):
            nc.sync.dma_start(out=raw_g[b][n][:, c],
                              in_=grad_out[b, n, c * D:(c + 1) * D, :].rearrange("(p j) w -> p j w", j=4))

        def load_top_whole(b):
            nc.sync.dma_start(out=raw_top[b][:],
                              in_=A1_atop_B1[b, 0].rearrange("(c p j) w -> p c j w", c=2, j=4))

        def load_g_whole(b, n):
            nc.sync.dma_start(out=raw_g[b][n][:],
                              in_=grad_out[b, n].rearrange("(c p j) w -> p c j w", c=2, j=4))

        load_top(0, 0)
        load_top(0, 1)
        load_g(0, 0, 1)
        load_g(0, 0, 0)
        load_top(1, 0)
        load_g(0, 1, 0)
        load_top(1, 1)
        load_g(0, 1, 1)

        ident = const.tile([P, P], F32, name="ident")
        make_identity(nc, ident[:])
        ident_bf = const.tile([P, P], BF16, name="ident_bf")
        make_identity(nc, ident_bf[:])
        junk = const.tile([P, W], BF16, name="junk")

        st = {}
        tl = {}

        def s_abs(b):
            st["abs", b] = scrp.tile([P, W], BF16, name="abs_a")
            st["sum", b] = small.tile([P, 1], F32, name="sum_a")
            nc.scalar.activation(out=st["abs", b][:], in_=raw_top[b][:, 0].rearrange("p j w -> p (j w)"),
                                 func=ACT.Abs, accum_out=st["sum", b][:])

        def v_nz(b):
            st["vs", b] = small.tile([P, 2], F32, name="vstat")
            nc.vector.tensor_scalar(out=junk[:], in0=raw_top[b][:, 1].rearrange("p j w -> p (j w)"), scalar1=0.0,
                                    scalar2=None, op0=ALU.not_equal, op1=ALU.max, accum_out=st["vs", b][:, 1:2])

        def v_mx(b):
            a = st["abs", b]
            nc.vector.tensor_scalar(out=a[:], in0=a[:], scalar1=1.0, scalar2=None, op0=ALU.mult,
                                    op1=ALU.max, accum_out=st["vs", b][:, 0:1])

        def pe_tr(b):
            ps = pstat.tile([P, 3, P], F32, name="ps")
            st["ps", b] = ps
            vs = st["vs", b]
            nc.tensor.transpose(out=ps[:, 0, :], in_=vs[:, 0:1].to_broadcast([P, P]), identity=ident[:])
            nc.tensor.transpose(out=ps[:, 1, :], in_=vs[:, 1:2].to_broadcast([P, P]), identity=ident[:])
            nc.tensor.transpose(out=ps[:, 2, :], in_=st["sum", b][:, 0:1].to_broadcast([P, P]), identity=ident[:])

        def v_red(b):
            ps = st["ps", b]
            st["red", b] = small.tile([P, 2], F32, name="red")
            nc.vector.tensor_reduce(out=st["red", b][:], in_=ps[:, 0:2, :], axis=AX.X, op=ALU.max)
            st["tot", b] = small.tile([P, 1], F32, name="tot")
            nc.vector.tensor_reduce(out=st["tot", b][:], in_=ps[:, 2, :], axis=AX.X, op=ALU.add)

        def v_u(b):
            st["u", b] = small.tile([P, 1], F32, name="u")
            nc.vector.tensor_scalar(out=st["u", b][:], in0=st["red", b][:, 1:2], scalar1=0.0,
                                    scalar2=st["tot", b][:, 0:1], op0=ALU.is_equal, op1=ALU.mult)

        def v_hg(b):
            st["h", b] = small.tile([P, 1], F32, name="h")
            nc.vector.tensor_scalar(out=st["h", b][:], in0=st["u", b][:], scalar1=float(D * D), scalar2=FLT_MAX,
                                    op0=ALU.is_gt, op1=ALU.mult)
            st["g", b] = small.tile([P, 1], F32, name="g")
            nc.vector.tensor_scalar(out=st["g", b][:], in0=st["u", b][:], scalar1=float(D * D), scalar2=None,
                                    op0=ALU.is_le)

        def v_den(b):
            st["den", b] = small.tile([P, 1], F32, name="den")
            nc.vector.scalar_tensor_tensor(out=st["den", b][:], in0=st["red", b][:, 0:1], scalar=st["h", b][:, 0:1],
                                           in1=st["g", b][:], op0=ALU.min, op1=ALU.max)

        def v_f(b):
            st["f", b] = small.tile([P, 1], F32, name="f")
            nc.vector.reciprocal(out=st["f", b][:], in_=st["den", b][:])

        def rg_top(b, c):
            grp = grpp.tile([P, 4, P, 4], BF16, name="grp_t", tag="grp", align_bytes=64)
            tl["gt", b, c] = grp
            dst = grp[:].rearrange("p m i j -> p i j m")
            src = raw_top[b][:, c].rearrange("p j (i m) -> p i j m", m=4)
            if c == 0:
                nc.vector.tensor_scalar(out=dst, in0=src, scalar1=st["f", b][:, 0:1], scalar2=None, op0=ALU.mult)
            else:
                nc.vector.tensor_copy(out=dst, in_=src)

        def q_top(b, c):
            if ("tq", b) not in tl:
                tl["tq", b] = topq.tile([P, 2, D], U32, name="tq", align_bytes=64)
                tl["ts", b] = topq.tile([P, 2, D], U8, name="ts", align_bytes=64)
            nc.vector.quantize_mx(out=tl["tq", b][:, c, :].bitcast(E4), scales=tl["ts", b][:, c, :],
                                  in_=tl["gt", b, c][:].rearrange("p m i j -> p (m i j)"))

        def rg_g(b, n, c, eng):
            if eng == "v":
                grp = grpp.tile([P, D, 4], BF16, name="grp_g", tag="grp", align_bytes=64)
            else:
                grp = grps.tile([P, D, 4], BF16, name="grp_s", align_bytes=64)
            tl["gg", b, n, c] = grp
            dst = grp[:].rearrange("p (c i) t -> p c t i", i=4)
            src = raw_g[b][n][:, c].rearrange("p t (c i) -> p c t i", i=4)
            if eng == "v":
                nc.vector.tensor_copy(out=dst, in_=src)
            else:
                nc.scalar.copy(out=dst, in_=src)

        def pe_rg(b, n, c):
            for h in range(2):
                ps = rgp.tile([P, 2, P, 4], BF16, name="ps_rg")
                tl["pr", b, n, c, h] = ps
                for q in range(2):
                    w0 = (2 * h + q) * P
                    nc.tensor.matmul(out=ps[:, q], lhsT=ident_bf[:],
                                     rhs=raw_g[b][n][:, c, :, w0:w0 + P].rearrange("p t w -> p w t"),
                                     start=True, stop=True)

        def s_rg(b, n, c):
            grp = grps.tile([P, D, 4], BF16, name="grp_s", align_bytes=64)
            tl["gg", b, n, c] = grp
            for h in range(2):
                nc.scalar.copy(out=grp[:, h * 2 * P:(h + 1) * 2 * P, :],
                               in_=tl["pr", b, n, c, h][:].rearrange("p q w t -> p (q w) t"))

        def q_g(b, n, c):
            if ("cq", b, n) not in tl:
                tl["cq", b, n] = gq.tile([P, 2, D], U32, name="cq", align_bytes=64)
                tl["cs", b, n] = gq.tile([P, 2, D], U8, name="cs", align_bytes=64)
            nc.vector.quantize_mx(out=tl["cq", b, n][:, c, :].bitcast(E5), scales=tl["cs", b, n][:, c, :],
                                  in_=tl["gg", b, n, c][:].rearrange("p w t -> p (w t)"))

        def cast(b, n, eng):
            ot = outp.tile([P, 4, D], F32, name="ot_c", tag="ot", align_bytes=256)
            if eng == "v":
                nc.vector.tensor_copy(out=ot[:], in_=raw_g[b][n][:, 1])
            else:
                nc.scalar.copy(out=ot[:], in_=raw_g[b][n][:, 1])
            tl["oc", b, n] = ot

        def cast_store(b, n, queue):
            queue.dma_start(out=out[b, n, D:2 * D, :].rearrange("(p j) w -> p j w", j=4), in_=tl["oc", b, n][:])

        def mm(b, n, order):
            tq, ts, cq, cs = tl["tq", b], tl["ts", b], tl["cq", b, n], tl["cs", b, n]
            for m in order:
                acc = accp.tile([P, D], F32, name="acc")
                tl["acc", b, n, m] = acc
                for k, c in enumerate((1, 0)):
                    nc.tensor.matmul_mx(
                        out=acc[:],
                        lhsT=tq[:, c, m * P:(m + 1) * P].bitcast(E4),
                        lhsT_scale=ts[:, c, m * P:(m + 1) * P],
                        rhs=cq[:, c, :].bitcast(E5),
                        rhs_scale=cs[:, c, :],
                        start=(k == 0),
                        stop=(k == 1),
                    )

        def evac(b, n):
            ot = outp.tile([P, 4, D], F32, name="ot_m", tag="ot", align_bytes=256)
            for m in range(4):
                nc.scalar.copy(out=ot[:, m, :], in_=tl["acc", b, n, m][:])
            nc.sync.dma_start(out=out[b, n, 0:D, :].rearrange("(i m) w -> i m w", m=4), in_=ot[:])

        def evac_last(b, n):
            dst = out[b, n, 0:D, :].rearrange("(i m) w -> i m w", m=4)
            o_s = outp.tile([P, 2, D], F32, name="ot_s", tag="ot", align_bytes=256)
            o_v = outp.tile([P, 2, D], F32, name="ot_v", tag="ot", align_bytes=256)
            nc.scalar.copy(out=o_s[:, 0, :], in_=tl["acc", b, n, 0][:])
            nc.vector.tensor_copy(out=o_v[:, 0, :], in_=tl["acc", b, n, 2][:])
            nc.scalar.copy(out=o_s[:, 1, :], in_=tl["acc", b, n, 1][:])
            nc.vector.tensor_copy(out=o_v[:, 1, :], in_=tl["acc", b, n, 3][:])
            nc.scalar.dma_start(out=dst[:, 0:2, :], in_=o_s[:])
            nc.sync.dma_start(out=dst[:, 2:4, :], in_=o_v[:])

        s_abs(0)
        v_nz(0)
        v_mx(0)
        pe_tr(0)
        cast(0, 0, "s")
        s_abs(1)
        cast_store(0, 0, nc.scalar)
        load_top_whole(2)
        load_g_whole(1, 0)
        load_g_whole(1, 1)
        load_g_whole(2, 0)
        rg_top(0, 1)
        v_red(0)
        rg_g(0, 0, 1, "v")
        v_u(0)
        q_top(0, 1)
        v_hg(0)
        rg_g(0, 0, 0, "v")
        v_den(0)
        q_g(0, 0, 1)
        v_f(0)
        q_g(0, 0, 0)
        rg_top(0, 0)
        v_nz(1)
        q_top(0, 0)
        v_mx(1)
        rg_g(0, 1, 0, "s")
        pe_tr(1)
        mm(0, 0, (0, 1, 2, 3))

        for s in range(1, 2 * B):
            b, n = s // 2, s % 2
            pb, pn = (s - 1) // 2, (s - 1) % 2
            last_b = b == B - 1
            if n == 0:
                s_rg(b, 0, 0)
                cast(b, 0, "s")
                evac(pb, pn)
                cast_store(b, 0, nc.scalar)
                rg_g(b, 0, 1, "v")
                rg_top(b, 0)
                q_g(b, 0, 1)
                if not last_b:
                    v_nz(b + 1)
                q_top(b, 0)
                if not last_b:
                    v_mx(b + 1)
                q_g(b, 0, 0)
                pe_rg(b, 1, 0)
                if not last_b:
                    pe_tr(b + 1)
                mm(b, 0, (0, 1, 2, 3))
            else:
                if b > 0:
                    s_rg(b, 1, 0)
                if b + 2 < B:
                    s_abs(b + 2)
                if not last_b:
                    cast(b, 1, "s")
                if s == 1:
                    cast_store(0, 1, nc.scalar)
                    load_top_whole(3)
                    load_g_whole(2, 1)
                evac(pb, pn)
                if s == 1:
                    load_g_whole(3, 0)
                    load_g_whole(3, 1)
                if 1 < s and not last_b:
                    cast_store(b, 1, nc.scalar)
                rg_g(b, 1, 1, "v")
                if not last_b:
                    v_red(b + 1)
                    rg_top(b + 1, 1)
                    v_u(b + 1)
                q_g(b, 1, 0)
                if not last_b:
                    v_hg(b + 1)
                q_g(b, 1, 1)
                if not last_b:
                    pe_rg(b + 1, 0, 0)
                mm(b, 1, (0, 2, 1, 3) if last_b else (0, 1, 2, 3))
                if not last_b:
                    v_den(b + 1)
                    q_top(b + 1, 1)
                    v_f(b + 1)
                else:
                    cast(b, 1, "v")
                    cast_store(b, 1, nc.scalar)
        evac_last(B - 1, 1)
